import numpy as np
import ml_dtypes


def mxq(x, axis, fmt="e4m3"):
    dtype, down = {"e4m3": (ml_dtypes.float8_e4m3fn, 7), "e5m2": (ml_dtypes.float8_e5m2, 14)}[fmt]
    v = np.moveaxis(np.asarray(x, np.float32).astype(ml_dtypes.bfloat16).astype(np.float64), axis, -1)
    blocks = v.reshape(v.shape[:-1] + (-1, 32))
    amax = np.abs(blocks).max(-1, keepdims=True)
    byte = np.maximum(np.where(amax > 0, np.frexp(amax)[1] - 1 + 127, 0) - down, 1)
    scale = np.exp2(byte - 127.0)
    codes = (blocks / scale).astype(np.float32).astype(dtype).astype(np.float64)
    return np.moveaxis((codes * scale).reshape(v.shape), -1, axis)


WIDE = False


def mx_kscale(k):
    if not WIDE:
        return np.ones(k)
    levels = np.array([10, -10, 5, -5, 0])
    if k % 512:
        return np.exp2(np.random.permutation(np.resize(levels, k // 32))).repeat(32)
    a = np.empty((k // 512, 16))
    for p in range(k // 512):
        a[p, :8] = np.random.permutation(np.resize(levels, 8))
        for g in range(8):
            far = levels[np.abs(levels - a[p, g]) >= 10]
            a[p, g + 8] = far[np.random.randint(len(far))]
    return np.exp2(a.ravel()).repeat(32)


BF16 = ml_dtypes.bfloat16


def bf(x):
    return np.asarray(x, np.float32).astype(BF16)


def f64(x):
    return np.asarray(x).astype(np.float64)


B, N, DIM, H, D, QB = 4, 2048, 1024, 2, 64, 512
E = H * D
RMS_EPS = 1e-12


def setup_inputs():
    s = mx_kscale(DIM)
    return {"x": bf(np.random.standard_normal((B, N, DIM))),
            "gamma": bf((1.0 + 0.1 * np.random.standard_normal(DIM)) * s),
            "w_qkv": bf(np.random.standard_normal((DIM, 3 * E)) * 1.5 / np.sqrt(DIM) / s[:, None])}


def reference(x, gamma, w_qkv):
    xf = f64(x)
    l2 = np.maximum(np.sqrt((xf * xf).sum(-1, keepdims=True)), RMS_EPS)
    normed = xf / l2 * np.sqrt(DIM) * f64(gamma)
    y = mxq(normed, 2, "e4m3") @ mxq(f64(w_qkv), 0, "e4m3")
    qkv = y.reshape(B, N, 3, H, D).transpose(2, 0, 3, 1, 4)
    return qkv[0] * D ** -0.5, qkv[1], qkv[2]

@@ -1,0 +1,223 @@
+from contextlib import ExitStack
+
+import concourse.mybir as mybir
+from concourse.masks import make_identity
+
+F32 = mybir.dt.float32
+BF16 = mybir.dt.bfloat16
+U32 = mybir.dt.uint32
+U8 = mybir.dt.uint8
+FP8X4 = mybir.dt.float8_e4m3fn_x4
+ALU = mybir.AluOpType
+ACT = mybir.ActivationFunctionType
+
+P = 128
+PACK = 4
+PAIR = 2
+K_PASS = P * PACK
+
+BATCH, SEQ, DIM, HEADS, HEAD_DIM = 4, 2048, 1024, 2, 64
+EMB = HEADS * HEAD_DIM
+COLS = 3 * EMB
+PASSES = DIM // K_PASS
+RMS_EPS = 1e-12
+N_TILES = BATCH * SEQ // P
+
+TILES_PER_STORE = 4
+TILES_PER_LOAD = 2
+STORES_PER_BATCH = SEQ // (P * TILES_PER_STORE)
+
+MOVING_COLS = 512
+
+FLOPS = 2 * BATCH * SEQ * DIM * COLS
+
+
+def quantise_weights(nc, setup, keep, w_raw):
+    w_grouped = setup.tile([P, PASSES, MOVING_COLS, PACK], BF16, align_bytes=64)
+    w_codes = keep.tile([P, PASSES, MOVING_COLS], U32, align_bytes=64)
+    w_scales = keep.tile([P, PASSES, MOVING_COLS], U8, align_bytes=64)
+    nc.vector.memset(w_grouped[:, :, COLS:MOVING_COLS, :], 0.0)
+    for g in range(PASSES):
+        nc.vector.tensor_copy(
+            out=w_grouped[:, g, 0:COLS, :], in_=w_raw[:, g].rearrange("p t n -> p n t")
+        )
+    for g in range(PASSES):
+        nc.vector.quantize_mx(
+            out=w_codes[:, g, :].bitcast(FP8X4),
+            scales=w_scales[:, g, :],
+            in_=w_grouped[:, g].rearrange("p n t -> p (n t)"),
+        )
+    return w_codes, w_scales
+
+
+SCALE_LAG = 3
+TURN_LAG = SCALE_LAG + 1
+REGROUP_LAG = TURN_LAG + 1
+QUANTISE_LAG = REGROUP_LAG + 1
+PROJECT_LAG = QUANTISE_LAG + 1
+EMIT_LAG = PROJECT_LAG + 1
+STORE_LAG = EMIT_LAG + 1
+LOADS_AHEAD = 3
+
+
+def tile_ringattention_pa_t_kernel(tc, x, gamma, w_qkv, out_0, out_1, out_2):
+    nc = tc.nc
+    x_groups = x.rearrange("b (c p s) k -> (b c) p s k", p=P, s=TILES_PER_STORE)
+    out_views = [
+        o.rearrange("b h (c p s) d -> b c p h s d", p=P, s=TILES_PER_STORE)
+        for o in (out_0, out_1, out_2)
+    ]
+    n_loads = N_TILES // TILES_PER_LOAD
+
+    with ExitStack() as ctx:
+        ctx.enter_context(tc.manual_schedule())
+        setup = ctx.enter_context(tc.tile_pool(name="setup", bufs=1))
+        keep = ctx.enter_context(tc.tile_pool(name="keep", bufs=1))
+        x_pool = ctx.enter_context(tc.tile_pool(name="x", bufs=2 * LOADS_AHEAD))
+        stat_pool = ctx.enter_context(tc.tile_pool(name="stat", bufs=4))
+        square_pool = ctx.enter_context(tc.tile_pool(name="square", bufs=2))
+        work = ctx.enter_context(tc.tile_pool(name="work", bufs=3))
+        y_pool = ctx.enter_context(tc.tile_pool(name="y", bufs=3))
+        psum_t = ctx.enter_context(tc.psum_pool(name="psum_t", bufs=3))
+        psum_y = ctx.enter_context(tc.psum_pool(name="psum_y", bufs=3))
+
+        x_sb, sum_sq, row_scale = {}, {}, {}
+        normed, turned, grouped, codes, scales, y_ps, y_sb = {}, {}, {}, {}, {}, {}, {}
+
+        def load_rows(h):
+            group, half = divmod(h, TILES_PER_STORE // TILES_PER_LOAD)
+            x_sb[h] = x_pool.tile([P, TILES_PER_LOAD, DIM], BF16, name="x_sb")
+            s0 = half * TILES_PER_LOAD
+            nc.sync.dma_start(out=x_sb[h][:], in_=x_groups[group][:, s0 : s0 + TILES_PER_LOAD, :])
+
+        def sum_squares(j):
+            h, s = divmod(j, TILES_PER_LOAD)
+            if s == 0:
+                sum_sq[h] = stat_pool.tile([P, TILES_PER_LOAD], F32, name="sum_sq")
+            squares = square_pool.tile([P, DIM], BF16)
+            nc.scalar.activation(
+                out=squares[:],
+                in_=x_sb[h][:, s, :],
+                func=ACT.Square,
+                accum_out=sum_sq[h][:, s : s + 1],
+            )
+            if s == TILES_PER_LOAD - 1:
+                unclamped = stat_pool.tile([P, TILES_PER_LOAD], F32)
+                nc.scalar.activation(
+                    out=unclamped[:],
+                    in_=sum_sq[h][:],
+                    func=ACT.Abs_reciprocal_sqrt,
+                    scale=1.0 / DIM,
+                )
+                row_scale[h] = stat_pool.tile([P, TILES_PER_LOAD], F32, name="row_scale")
+                nc.gpsimd.tensor_scalar_min(
+                    out=row_scale[h][:], in0=unclamped[:], scalar1=DIM**0.5 / RMS_EPS
+                )
+
+        def scale_rows(j):
+            h, s = divmod(j, TILES_PER_LOAD)
+            normed[j] = work.tile([P, DIM], BF16, name="normed")
+            nc.vector.scalar_tensor_tensor(
+                out=normed[j][:],
+                in0=x_sb[h][:, s, :],
+                scalar=row_scale[h][:, s : s + 1],
+                in1=gamma_all[:],
+                op0=ALU.mult,
+                op1=ALU.mult,
+            )
+
+        def turn(j):
+            words = normed[j][:].bitcast(F32)
+            turned[j] = psum_t.tile([P, PASSES, PAIR, P], F32, name="turned")
+            for g in range(PASSES):
+                for u in range(PAIR):
+                    w0 = g * PAIR * P
+                    nc.tensor.transpose(
+                        out=turned[j][:, g, u, :],
+                        in_=words[:, w0 + u : w0 + PAIR * P : PAIR],
+                        identity=identity[:],
+                    )
+
+        def regroup(j):
+            grouped[j] = work.tile([P, PASSES, P, PAIR], F32, name="grouped", align_bytes=64)
+            nc.scalar.copy(out=grouped[j][:], in_=turned[j][:].rearrange("p g u i -> p g i u"))
+
+        def quantise(j):
+            codes[j] = work.tile([P, PASSES, P], U32, name="codes", align_bytes=64)
+            scales[j] = work.tile([P, PASSES, P], U8, name="scales", align_bytes=64)
+            nc.vector.quantize_mx(
+                out=codes[j][:].rearrange("p g i -> p (g i)").bitcast(FP8X4),
+                scales=scales[j][:].rearrange("p g i -> p (g i)"),
+                in_=grouped[j][:].rearrange("p g i u -> p (g i u)").bitcast(BF16),
+            )
+
+        def project(j):
+            y_ps[j] = psum_y.tile([P, MOVING_COLS], F32, name="y_ps")
+            for g in range(PASSES):
+                nc.tensor.matmul_mx(
+                    out=y_ps[j][:],
+                    lhsT=codes[j][:, g, :].bitcast(FP8X4),
+                    lhsT_scale=scales[j][:, g, :],
+                    rhs=w_codes[:, g, :].bitcast(FP8X4),
+                    rhs_scale=w_scales[:, g, :],
+                    start=(g == 0),
+                    stop=(g == PASSES - 1),
+                )
+
+        def emit(j):
+            group, s = divmod(j, TILES_PER_STORE)
+            if s == 0:
+                y_sb[group] = y_pool.tile(
+                    [P, 3, HEADS, TILES_PER_STORE, HEAD_DIM], F32, name="y_sb"
+                )
+            nc.vector.tensor_scalar_mul(
+                out=y_sb[group][:, 0, :, s, :],
+                in0=y_ps[j][:, 0:EMB].rearrange("p (h d) -> p h d", h=HEADS),
+                scalar1=HEAD_DIM**-0.5,
+            )
+            nc.vector.tensor_copy(
+                out=y_sb[group][:, 1:3, :, s, :],
+                in_=y_ps[j][:, EMB:COLS].rearrange("p (j h d) -> p j h d", j=2, h=HEADS),
+            )
+
+        def store(group):
+            b, c = divmod(group, STORES_PER_BATCH)
+            for tensor in range(3):
+                nc.sync.dma_start(out=out_views[tensor][b, c], in_=y_sb[group][:, tensor])
+
+        w_raw = setup.tile([P, PASSES, PACK, COLS], BF16)
+        nc.sync.dma_start(
+            out=w_raw[:].rearrange("p g t n -> p g (t n)"),
+            in_=w_qkv.rearrange("(g p t) n -> p g (t n)", p=P, t=PACK),
+        )
+        load_rows(0)
+        gamma_all = keep.tile([P, DIM], BF16)
+        nc.sync.dma_start(out=gamma_all[:], in_=gamma.partition_broadcast(P))
+        for h in range(1, LOADS_AHEAD):
+            load_rows(h)
+        identity = keep.tile([P, P], F32)
+        make_identity(nc, identity[:])
+        w_codes, w_scales = quantise_weights(nc, setup, keep, w_raw)
+
+        def due(j):
+            return 0 <= j < N_TILES
+
+        for step in range(N_TILES + STORE_LAG):
+            if step % TILES_PER_LOAD == 0 and step // TILES_PER_LOAD + LOADS_AHEAD < n_loads:
+                load_rows(step // TILES_PER_LOAD + LOADS_AHEAD)
+            if due(step - STORE_LAG) and (step - STORE_LAG) % TILES_PER_STORE == TILES_PER_STORE - 1:
+                store((step - STORE_LAG) // TILES_PER_STORE)
+            if due(step - EMIT_LAG):
+                emit(step - EMIT_LAG)
+            if due(step - PROJECT_LAG):
+                project(step - PROJECT_LAG)
+            if due(step - QUANTISE_LAG):
+                quantise(step - QUANTISE_LAG)
+            if due(step - REGROUP_LAG):
+                regroup(step - REGROUP_LAG)
+            if due(step - TURN_LAG):
+                turn(step - TURN_LAG)
+            if due(step - SCALE_LAG):
+                scale_rows(step - SCALE_LAG)
+            if due(step):
+                sum_squares(step)

@@ -51,6 +51,7 @@ def quantise_weights(nc, setup, keep, w_raw):
 
 
 SCALE_LAG = 3
+INVERT_LAG = 1
 TURN_LAG = SCALE_LAG + 1
 REGROUP_LAG = TURN_LAG + 1
 QUANTISE_LAG = REGROUP_LAG + 1
@@ -101,18 +102,19 @@ def tile_ringattention_pa_t_kernel(tc, x, gamma, w_qkv, out_0, out_1, out_2):
                 func=ACT.Square,
                 accum_out=sum_sq[h][:, s : s + 1],
             )
-            if s == TILES_PER_LOAD - 1:
-                unclamped = stat_pool.tile([P, TILES_PER_LOAD], F32)
-                nc.scalar.activation(
-                    out=unclamped[:],
-                    in_=sum_sq[h][:],
-                    func=ACT.Abs_reciprocal_sqrt,
-                    scale=1.0 / DIM,
-                )
-                row_scale[h] = stat_pool.tile([P, TILES_PER_LOAD], F32, name="row_scale")
-                nc.gpsimd.tensor_scalar_min(
-                    out=row_scale[h][:], in0=unclamped[:], scalar1=DIM**0.5 / RMS_EPS
-                )
+
+        def invert_norms(h):
+            unclamped = stat_pool.tile([P, TILES_PER_LOAD], F32)
+            nc.scalar.activation(
+                out=unclamped[:],
+                in_=sum_sq[h][:],
+                func=ACT.Abs_reciprocal_sqrt,
+                scale=1.0 / DIM,
+            )
+            row_scale[h] = stat_pool.tile([P, TILES_PER_LOAD], F32, name="row_scale")
+            nc.gpsimd.tensor_scalar_min(
+                out=row_scale[h][:], in0=unclamped[:], scalar1=DIM**0.5 / RMS_EPS
+            )
 
         def scale_rows(j):
             h, s = divmod(j, TILES_PER_LOAD)
@@ -195,6 +197,10 @@ def tile_ringattention_pa_t_kernel(tc, x, gamma, w_qkv, out_0, out_1, out_2):
         nc.sync.dma_start(out=gamma_all[:], in_=gamma.partition_broadcast(P))
         for h in range(1, LOADS_AHEAD):
             load_rows(h)
+        one = stat_pool.tile([P, 1], F32)
+        nc.vector.memset(one[:], 1.0)
+        warm = stat_pool.tile([P, 1], F32)
+        nc.scalar.activation(out=warm[:], in_=one[:], func=ACT.Abs_reciprocal_sqrt)
         identity = keep.tile([P, P], F32)
         make_identity(nc, identity[:])
         w_codes, w_scales = quantise_weights(nc, setup, keep, w_raw)
@@ -219,5 +225,7 @@ def tile_ringattention_pa_t_kernel(tc, x, gamma, w_qkv, out_0, out_1, out_2):
                 turn(step - TURN_LAG)
             if due(step - SCALE_LAG):
                 scale_rows(step - SCALE_LAG)
+            if due(step - INVERT_LAG) and (step - INVERT_LAG) % TILES_PER_LOAD == TILES_PER_LOAD - 1:
+                invert_norms((step - INVERT_LAG) // TILES_PER_LOAD)
             if due(step):
                 sum_squares(step)

@@ -28,6 +28,7 @@ TILES_PER_LOAD = 2
 STORES_PER_BATCH = SEQ // (P * TILES_PER_STORE)
 
 MOVING_COLS = 512
+BANK = 512
 
 FLOPS = 2 * BATCH * SEQ * DIM * COLS
 
@@ -50,15 +51,16 @@ def quantise_weights(nc, setup, keep, w_raw):
     return w_codes, w_scales
 
 
-SCALE_LAG = 3
 INVERT_LAG = 1
+CLAMP_LAG = 2
+SCALE_LAG = CLAMP_LAG + 1
 TURN_LAG = SCALE_LAG + 1
 REGROUP_LAG = TURN_LAG + 1
-QUANTISE_LAG = REGROUP_LAG + 1
+QUANTISE_LAG = REGROUP_LAG + 2
 PROJECT_LAG = QUANTISE_LAG + 1
 EMIT_LAG = PROJECT_LAG + 1
 STORE_LAG = EMIT_LAG + 1
-LOADS_AHEAD = 3
+LOADS_AHEAD = 4
 
 
 def tile_ringattention_pa_t_kernel(tc, x, gamma, w_qkv, out_0, out_1, out_2):
@@ -77,13 +79,14 @@ def tile_ringattention_pa_t_kernel(tc, x, gamma, w_qkv, out_0, out_1, out_2):
         x_pool = ctx.enter_context(tc.tile_pool(name="x", bufs=2 * LOADS_AHEAD))
         stat_pool = ctx.enter_context(tc.tile_pool(name="stat", bufs=4))
         square_pool = ctx.enter_context(tc.tile_pool(name="square", bufs=2))
-        work = ctx.enter_context(tc.tile_pool(name="work", bufs=3))
+        work = ctx.enter_context(tc.tile_pool(name="work", bufs=5))
         y_pool = ctx.enter_context(tc.tile_pool(name="y", bufs=3))
-        psum_t = ctx.enter_context(tc.psum_pool(name="psum_t", bufs=3))
+        psum_g = ctx.enter_context(tc.psum_pool(name="psum_g", bufs=1))
+        psum_t = ctx.enter_context(tc.psum_pool(name="psum_t", bufs=4))
         psum_y = ctx.enter_context(tc.psum_pool(name="psum_y", bufs=3))
 
-        x_sb, sum_sq, row_scale = {}, {}, {}
-        normed, turned, grouped, codes, scales, y_ps, y_sb = {}, {}, {}, {}, {}, {}, {}
+        x_sb, sum_sq, unclamped, row_scale = {}, {}, {}, {}
+        scaled, normed, turned, grouped, codes, scales, y_ps, y_sb = ({} for i in range(8))
 
         def load_rows(h):
             group, half = divmod(h, TILES_PER_STORE // TILES_PER_LOAD)
@@ -104,45 +107,87 @@ def tile_ringattention_pa_t_kernel(tc, x, gamma, w_qkv, out_0, out_1, out_2):
             )
 
         def invert_norms(h):
-            unclamped = stat_pool.tile([P, TILES_PER_LOAD], F32)
+            unclamped[h] = stat_pool.tile([P, TILES_PER_LOAD], F32, name="unclamped")
             nc.scalar.activation(
-                out=unclamped[:],
+                out=unclamped[h][:],
                 in_=sum_sq[h][:],
                 func=ACT.Abs_reciprocal_sqrt,
                 scale=1.0 / DIM,
             )
+
+        def clamp(h):
             row_scale[h] = stat_pool.tile([P, TILES_PER_LOAD], F32, name="row_scale")
-            nc.gpsimd.tensor_scalar_min(
-                out=row_scale[h][:], in0=unclamped[:], scalar1=DIM**0.5 / RMS_EPS
+            nc.vector.tensor_scalar_min(
+                out=row_scale[h][:], in0=unclamped[h][:], scalar1=DIM**0.5 / RMS_EPS
             )
 
-        def scale_rows(j):
+        def scale_even(j):
+            h, s = divmod(j, TILES_PER_LOAD)
+            scaled[j] = work.tile([P, PACK, DIM // PACK], F32, name="scaled")
+            nc.gpsimd.tensor_scalar(
+                out=scaled[j][:],
+                in0=x_sb[h][:, s, :].rearrange("p (w t) -> p t w", t=PACK),
+                scalar1=row_scale[h][:, s : s + 1],
+                scalar2=0.0,
+                op0=ALU.mult,
+                op1=ALU.add,
+            )
+
+        def scale_odd(j):
             h, s = divmod(j, TILES_PER_LOAD)
             normed[j] = work.tile([P, DIM], BF16, name="normed")
             nc.vector.scalar_tensor_tensor(
                 out=normed[j][:],
                 in0=x_sb[h][:, s, :],
                 scalar=row_scale[h][:, s : s + 1],
-                in1=gamma_all[:],
+                in1=gamma_ps[:],
                 op0=ALU.mult,
                 op1=ALU.mult,
             )
 
-        def turn(j):
+        def turn_even(j):
+            turned[j] = []
+            for g in range(PASSES):
+                bank = psum_t.tile([P, PACK, P], F32, name="turned_bank")
+                for t in range(PACK):
+                    nc.tensor.transpose(
+                        out=bank[:, t, :],
+                        in_=scaled[j][:, t, g * P : (g + 1) * P],
+                        identity=identity[:],
+                    )
+                turned[j].append(bank)
+
+        def turn_odd(j):
             words = normed[j][:].bitcast(F32)
-            turned[j] = psum_t.tile([P, PASSES, PAIR, P], F32, name="turned")
+            bank = psum_t.tile([P, PACK, P], F32, name="turned_bank")
             for g in range(PASSES):
                 for u in range(PAIR):
                     w0 = g * PAIR * P
                     nc.tensor.transpose(
-                        out=turned[j][:, g, u, :],
+                        out=bank[:, g * PAIR + u, :],
                         in_=words[:, w0 + u : w0 + PAIR * P : PAIR],
                         identity=identity[:],
                     )
+            turned[j] = bank
 
-        def regroup(j):
-            grouped[j] = work.tile([P, PASSES, P, PAIR], F32, name="grouped", align_bytes=64)
-            nc.scalar.copy(out=grouped[j][:], in_=turned[j][:].rearrange("p g u i -> p g i u"))
+        def regroup_even(j):
+            grouped[j] = work.tile([P, PASSES, P, PACK], BF16, name="grouped", align_bytes=64)
+            for g in range(PASSES):
+                nc.vector.tensor_tensor(
+                    out=grouped[j][:, g],
+                    in0=turned[j][g][:].rearrange("p t i -> p i t"),
+                    in1=gamma_turned[:, g, :].unsqueeze(1).to_broadcast([P, P, PACK]),
+                    op=ALU.mult,
+                )
+
+        def regroup_odd(j):
+            grouped[j] = work.tile([P, PASSES, P, PACK], BF16, name="grouped", align_bytes=64)
+            nc.scalar.copy(
+                out=grouped[j][:].rearrange("p g i t -> p g (i t)").bitcast(F32).rearrange(
+                    "p g (i u) -> p g i u", u=PAIR
+                ),
+                in_=turned[j][:].rearrange("p (g u) i -> p g i u", u=PAIR),
+            )
 
         def quantise(j):
             codes[j] = work.tile([P, PASSES, P], U32, name="codes", align_bytes=64)
@@ -150,7 +195,7 @@ def tile_ringattention_pa_t_kernel(tc, x, gamma, w_qkv, out_0, out_1, out_2):
             nc.vector.quantize_mx(
                 out=codes[j][:].rearrange("p g i -> p (g i)").bitcast(FP8X4),
                 scales=scales[j][:].rearrange("p g i -> p (g i)"),
-                in_=grouped[j][:].rearrange("p g i u -> p (g i u)").bitcast(BF16),
+                in_=grouped[j][:].rearrange("p g i t -> p (g i t)"),
             )
 
         def project(j):
@@ -172,15 +217,16 @@ def tile_ringattention_pa_t_kernel(tc, x, gamma, w_qkv, out_0, out_1, out_2):
                 y_sb[group] = y_pool.tile(
                     [P, 3, HEADS, TILES_PER_STORE, HEAD_DIM], F32, name="y_sb"
                 )
-            nc.vector.tensor_scalar_mul(
-                out=y_sb[group][:, 0, :, s, :],
-                in0=y_ps[j][:, 0:EMB].rearrange("p (h d) -> p h d", h=HEADS),
-                scalar1=HEAD_DIM**-0.5,
-            )
-            nc.vector.tensor_copy(
-                out=y_sb[group][:, 1:3, :, s, :],
-                in_=y_ps[j][:, EMB:COLS].rearrange("p (j h d) -> p j h d", j=2, h=HEADS),
-            )
+            q_out = y_sb[group][:, 0, :, s, :]
+            q_in = y_ps[j][:, 0:EMB].rearrange("p (h d) -> p h d", h=HEADS)
+            kv_out = y_sb[group][:, 1:3, :, s, :]
+            kv_in = y_ps[j][:, EMB:COLS].rearrange("p (j h d) -> p j h d", j=2, h=HEADS)
+            if j % 2 == 0:
+                nc.vector.tensor_scalar_mul(out=q_out, in0=q_in, scalar1=HEAD_DIM**-0.5)
+                nc.vector.tensor_copy(out=kv_out, in_=kv_in)
+            else:
+                nc.scalar.mul(out=q_out, in_=q_in, mul=HEAD_DIM**-0.5)
+                nc.scalar.copy(out=kv_out, in_=kv_in)
 
         def store(group):
             b, c = divmod(group, STORES_PER_BATCH)
@@ -193,8 +239,12 @@ def tile_ringattention_pa_t_kernel(tc, x, gamma, w_qkv, out_0, out_1, out_2):
             in_=w_qkv.rearrange("(g p t) n -> p g (t n)", p=P, t=PACK),
         )
         load_rows(0)
-        gamma_all = keep.tile([P, DIM], BF16)
+        gamma_all = setup.tile([P, DIM], BF16)
         nc.sync.dma_start(out=gamma_all[:], in_=gamma.partition_broadcast(P))
+        gamma_turned = keep.tile([P, PASSES, PACK], BF16)
+        nc.sync.dma_start(
+            out=gamma_turned[:], in_=gamma.rearrange("(g p t) -> p g t", p=P, t=PACK)
+        )
         for h in range(1, LOADS_AHEAD):
             load_rows(h)
         one = stat_pool.tile([P, 1], F32)
@@ -203,6 +253,17 @@ def tile_ringattention_pa_t_kernel(tc, x, gamma, w_qkv, out_0, out_1, out_2):
         nc.scalar.activation(out=warm[:], in_=one[:], func=ACT.Abs_reciprocal_sqrt)
         identity = keep.tile([P, P], F32)
         make_identity(nc, identity[:])
+        identity_bf16 = setup.tile([P, P], BF16)
+        nc.vector.tensor_copy(out=identity_bf16[:], in_=identity[:])
+        gamma_ps = psum_g.tile([P, DIM], BF16)
+        for c in range(0, DIM, BANK):
+            nc.tensor.matmul(
+                gamma_ps[:, c : c + BANK],
+                lhsT=identity_bf16[:],
+                rhs=gamma_all[:, c : c + BANK],
+                start=True,
+                stop=True,
+            )
         w_codes, w_scales = quantise_weights(nc, setup, keep, w_raw)
 
         def due(j):
@@ -213,18 +274,23 @@ def tile_ringattention_pa_t_kernel(tc, x, gamma, w_qkv, out_0, out_1, out_2):
                 load_rows(step // TILES_PER_LOAD + LOADS_AHEAD)
             if due(step - STORE_LAG) and (step - STORE_LAG) % TILES_PER_STORE == TILES_PER_STORE - 1:
                 store((step - STORE_LAG) // TILES_PER_STORE)
+            if due(step - QUANTISE_LAG):
+                quantise(step - QUANTISE_LAG)
+            if due(step - CLAMP_LAG) and (step - CLAMP_LAG) % TILES_PER_LOAD == TILES_PER_LOAD - 1:
+                clamp((step - CLAMP_LAG) // TILES_PER_LOAD)
             if due(step - EMIT_LAG):
                 emit(step - EMIT_LAG)
             if due(step - PROJECT_LAG):
                 project(step - PROJECT_LAG)
-            if due(step - QUANTISE_LAG):
-                quantise(step - QUANTISE_LAG)
             if due(step - REGROUP_LAG):
-                regroup(step - REGROUP_LAG)
+                j = step - REGROUP_LAG
+                (regroup_odd if j % 2 else regroup_even)(j)
             if due(step - TURN_LAG):
-                turn(step - TURN_LAG)
+                j = step - TURN_LAG
+                (turn_odd if j % 2 else turn_even)(j)
             if due(step - SCALE_LAG):
-                scale_rows(step - SCALE_LAG)
+                j = step - SCALE_LAG
+                (scale_odd if j % 2 else scale_even)(j)
             if due(step - INVERT_LAG) and (step - INVERT_LAG) % TILES_PER_LOAD == TILES_PER_LOAD - 1:
                 invert_norms((step - INVERT_LAG) // TILES_PER_LOAD)
             if due(step):

@@ -85,8 +85,15 @@ def tile_ringattention_pa_t_kernel(tc, x, gamma, w_qkv, out_0, out_1, out_2):
         psum_t = ctx.enter_context(tc.psum_pool(name="psum_t", bufs=4))
         psum_y = ctx.enter_context(tc.psum_pool(name="psum_y", bufs=3))
 
-        x_sb, sum_sq, unclamped, row_scale = {}, {}, {}, {}
+        x_sb = {}
         scaled, normed, turned, grouped, codes, scales, y_ps, y_sb = ({} for i in range(8))
+
+        sum_sq = keep.tile([P, N_TILES], F32)
+        unclamped = keep.tile([P, N_TILES], F32)
+        row_scale = keep.tile([P, N_TILES], F32)
+
+        def rows_of(h):
+            return slice(h * TILES_PER_LOAD, (h + 1) * TILES_PER_LOAD)
 
         def load_rows(h):
             group, half = divmod(h, TILES_PER_STORE // TILES_PER_LOAD)
@@ -96,29 +103,27 @@ def tile_ringattention_pa_t_kernel(tc, x, gamma, w_qkv, out_0, out_1, out_2):
 
         def sum_squares(j):
             h, s = divmod(j, TILES_PER_LOAD)
-            if s == 0:
-                sum_sq[h] = stat_pool.tile([P, TILES_PER_LOAD], F32, name="sum_sq")
             squares = square_pool.tile([P, DIM], BF16)
             nc.scalar.activation(
                 out=squares[:],
                 in_=x_sb[h][:, s, :],
                 func=ACT.Square,
-                accum_out=sum_sq[h][:, s : s + 1],
+                accum_out=sum_sq[:, j : j + 1],
             )
 
         def invert_norms(h):
-            unclamped[h] = stat_pool.tile([P, TILES_PER_LOAD], F32, name="unclamped")
             nc.scalar.activation(
-                out=unclamped[h][:],
-                in_=sum_sq[h][:],
+                out=unclamped[:, rows_of(h)],
+                in_=sum_sq[:, rows_of(h)],
                 func=ACT.Abs_reciprocal_sqrt,
                 scale=1.0 / DIM,
             )
 
         def clamp(h):
-            row_scale[h] = stat_pool.tile([P, TILES_PER_LOAD], F32, name="row_scale")
             nc.vector.tensor_scalar_min(
-                out=row_scale[h][:], in0=unclamped[h][:], scalar1=DIM**0.5 / RMS_EPS
+                out=row_scale[:, rows_of(h)],
+                in0=unclamped[:, rows_of(h)],
+                scalar1=DIM**0.5 / RMS_EPS,
             )
 
         def scale_even(j):
@@ -127,7 +132,7 @@ def tile_ringattention_pa_t_kernel(tc, x, gamma, w_qkv, out_0, out_1, out_2):
             nc.gpsimd.tensor_scalar(
                 out=scaled[j][:],
                 in0=x_sb[h][:, s, :].rearrange("p (w t) -> p t w", t=PACK),
-                scalar1=row_scale[h][:, s : s + 1],
+                scalar1=row_scale[:, j : j + 1],
                 scalar2=0.0,
                 op0=ALU.mult,
                 op1=ALU.add,
@@ -139,7 +144,7 @@ def tile_ringattention_pa_t_kernel(tc, x, gamma, w_qkv, out_0, out_1, out_2):
             nc.vector.scalar_tensor_tensor(
                 out=normed[j][:],
                 in0=x_sb[h][:, s, :],
-                scalar=row_scale[h][:, s : s + 1],
+                scalar=row_scale[:, j : j + 1],
                 in1=gamma_ps[:],
                 op0=ALU.mult,
                 op1=ALU.mult,
@@ -222,8 +227,12 @@ def tile_ringattention_pa_t_kernel(tc, x, gamma, w_qkv, out_0, out_1, out_2):
             kv_out = y_sb[group][:, 1:3, :, s, :]
             kv_in = y_ps[j][:, EMB:COLS].rearrange("p (j h d) -> p j h d", j=2, h=HEADS)
             if j % 2 == 0:
-                nc.vector.tensor_scalar_mul(out=q_out, in0=q_in, scalar1=HEAD_DIM**-0.5)
-                nc.vector.tensor_copy(out=kv_out, in_=kv_in)
+                nc.vector.tensor_tensor(
+                    out=y_sb[group][:, :, :, s, :],
+                    in0=y_ps[j][:, 0:COLS].rearrange("p (j h d) -> p j h d", j=3, h=HEADS),
+                    in1=y_factor[:].rearrange("p (j h d) -> p j h d", j=3, h=HEADS),
+                    op=ALU.mult,
+                )
             else:
                 nc.scalar.mul(out=q_out, in_=q_in, mul=HEAD_DIM**-0.5)
                 nc.scalar.copy(out=kv_out, in_=kv_in)
@@ -264,6 +273,9 @@ def tile_ringattention_pa_t_kernel(tc, x, gamma, w_qkv, out_0, out_1, out_2):
                 start=True,
                 stop=True,
             )
+        y_factor = keep.tile([P, COLS], F32)
+        nc.gpsimd.memset(y_factor[:, 0:EMB], HEAD_DIM**-0.5)
+        nc.gpsimd.memset(y_factor[:, EMB:COLS], 1.0)
         w_codes, w_scales = quantise_weights(nc, setup, keep, w_raw)
 
         def due(j):

@@ -33,34 +33,20 @@ BANK = 512
 FLOPS = 2 * BATCH * SEQ * DIM * COLS
 
 
-def quantise_weights(nc, setup, keep, w_raw):
-    w_grouped = setup.tile([P, PASSES, MOVING_COLS, PACK], BF16, align_bytes=64)
-    w_codes = keep.tile([P, PASSES, MOVING_COLS], U32, align_bytes=64)
-    w_scales = keep.tile([P, PASSES, MOVING_COLS], U8, align_bytes=64)
-    nc.vector.memset(w_grouped[:, :, COLS:MOVING_COLS, :], 0.0)
-    for g in range(PASSES):
-        nc.vector.tensor_copy(
-            out=w_grouped[:, g, 0:COLS, :], in_=w_raw[:, g].rearrange("p t n -> p n t")
-        )
-    for g in range(PASSES):
-        nc.vector.quantize_mx(
-            out=w_codes[:, g, :].bitcast(FP8X4),
-            scales=w_scales[:, g, :],
-            in_=w_grouped[:, g].rearrange("p n t -> p (n t)"),
-        )
-    return w_codes, w_scales
-
+VECTOR_TILE = 2
+QUANTISE_SIZES = [4] * (N_TILES // 4 - 1) + [1] * 4
 
 INVERT_LAG = 1
-CLAMP_LAG = 2
+CLAMP_LAG = 3
 SCALE_LAG = CLAMP_LAG + 1
 TURN_LAG = SCALE_LAG + 1
-REGROUP_LAG = TURN_LAG + 1
+REGROUP_LAG = TURN_LAG + 2
 QUANTISE_LAG = REGROUP_LAG + 2
-PROJECT_LAG = QUANTISE_LAG + 1
+PROJECT_LAG = QUANTISE_LAG + 4
 EMIT_LAG = PROJECT_LAG + 1
 STORE_LAG = EMIT_LAG + 1
-LOADS_AHEAD = 4
+WEIGHT_STEPS = (4, 5, 9)
+LOADS_AHEAD = 6
 
 
 def tile_ringattention_pa_t_kernel(tc, x, gamma, w_qkv, out_0, out_1, out_2):
@@ -76,10 +62,9 @@ def tile_ringattention_pa_t_kernel(tc, x, gamma, w_qkv, out_0, out_1, out_2):
         ctx.enter_context(tc.manual_schedule())
         setup = ctx.enter_context(tc.tile_pool(name="setup", bufs=1))
         keep = ctx.enter_context(tc.tile_pool(name="keep", bufs=1))
-        x_pool = ctx.enter_context(tc.tile_pool(name="x", bufs=2 * LOADS_AHEAD))
-        stat_pool = ctx.enter_context(tc.tile_pool(name="stat", bufs=4))
+        x_pool = ctx.enter_context(tc.tile_pool(name="x", bufs=LOADS_AHEAD + 6))
         square_pool = ctx.enter_context(tc.tile_pool(name="square", bufs=2))
-        work = ctx.enter_context(tc.tile_pool(name="work", bufs=5))
+        work = ctx.enter_context(tc.tile_pool(name="work", bufs=4))
         y_pool = ctx.enter_context(tc.tile_pool(name="y", bufs=3))
         psum_g = ctx.enter_context(tc.psum_pool(name="psum_g", bufs=1))
         psum_t = ctx.enter_context(tc.psum_pool(name="psum_t", bufs=4))
@@ -99,7 +84,13 @@ def tile_ringattention_pa_t_kernel(tc, x, gamma, w_qkv, out_0, out_1, out_2):
             group, half = divmod(h, TILES_PER_STORE // TILES_PER_LOAD)
             x_sb[h] = x_pool.tile([P, TILES_PER_LOAD, DIM], BF16, name="x_sb")
             s0 = half * TILES_PER_LOAD
-            nc.sync.dma_start(out=x_sb[h][:], in_=x_groups[group][:, s0 : s0 + TILES_PER_LOAD, :])
+            pieces = TILES_PER_LOAD if h == 0 else 1
+            size = TILES_PER_LOAD // pieces
+            for s in range(0, TILES_PER_LOAD, size):
+                nc.sync.dma_start(
+                    out=x_sb[h][:, s : s + size, :],
+                    in_=x_groups[group][:, s0 + s : s0 + s + size, :],
+                )
 
         def sum_squares(j):
             h, s = divmod(j, TILES_PER_LOAD)
@@ -126,7 +117,7 @@ def tile_ringattention_pa_t_kernel(tc, x, gamma, w_qkv, out_0, out_1, out_2):
                 scalar1=DIM**0.5 / RMS_EPS,
             )
 
-        def scale_even(j):
+        def scale_on_gpsimd(j):
             h, s = divmod(j, TILES_PER_LOAD)
             scaled[j] = work.tile([P, PACK, DIM // PACK], F32, name="scaled")
             nc.gpsimd.tensor_scalar(
@@ -138,7 +129,7 @@ def tile_ringattention_pa_t_kernel(tc, x, gamma, w_qkv, out_0, out_1, out_2):
                 op1=ALU.add,
             )
 
-        def scale_odd(j):
+        def scale_on_vector(j):
             h, s = divmod(j, TILES_PER_LOAD)
             normed[j] = work.tile([P, DIM], BF16, name="normed")
             nc.vector.scalar_tensor_tensor(
@@ -150,7 +141,7 @@ def tile_ringattention_pa_t_kernel(tc, x, gamma, w_qkv, out_0, out_1, out_2):
                 op1=ALU.mult,
             )
 
-        def turn_even(j):
+        def turn_values(j):
             turned[j] = []
             for g in range(PASSES):
                 bank = psum_t.tile([P, PACK, P], F32, name="turned_bank")
@@ -162,7 +153,7 @@ def tile_ringattention_pa_t_kernel(tc, x, gamma, w_qkv, out_0, out_1, out_2):
                     )
                 turned[j].append(bank)
 
-        def turn_odd(j):
+        def turn_words(j):
             words = normed[j][:].bitcast(F32)
             bank = psum_t.tile([P, PACK, P], F32, name="turned_bank")
             for g in range(PASSES):
@@ -175,41 +166,50 @@ def tile_ringattention_pa_t_kernel(tc, x, gamma, w_qkv, out_0, out_1, out_2):
                     )
             turned[j] = bank
 
-        def regroup_even(j):
-            grouped[j] = work.tile([P, PASSES, P, PACK], BF16, name="grouped", align_bytes=64)
+        def open_group(j):
+            if j % TILES_PER_STORE == 0:
+                c = j // TILES_PER_STORE
+                shape = [P, TILES_PER_STORE, PASSES, P]
+                grouped[c] = work.tile(shape + [PACK], BF16, name="grouped", align_bytes=64)
+                codes[c] = work.tile(shape, U32, name="codes", align_bytes=64)
+                scales[c] = work.tile(shape, U8, name="scales", align_bytes=64)
+
+        def regroup_times_gamma(j):
+            c, s = divmod(j, TILES_PER_STORE)
             for g in range(PASSES):
                 nc.vector.tensor_tensor(
-                    out=grouped[j][:, g],
+                    out=grouped[c][:, s, g],
                     in0=turned[j][g][:].rearrange("p t i -> p i t"),
                     in1=gamma_turned[:, g, :].unsqueeze(1).to_broadcast([P, P, PACK]),
                     op=ALU.mult,
                 )
 
-        def regroup_odd(j):
-            grouped[j] = work.tile([P, PASSES, P, PACK], BF16, name="grouped", align_bytes=64)
+        def regroup_words(j):
+            c, s = divmod(j, TILES_PER_STORE)
             nc.scalar.copy(
-                out=grouped[j][:].rearrange("p g i t -> p g (i t)").bitcast(F32).rearrange(
+                out=grouped[c][:, s].rearrange("p g i t -> p g (i t)").bitcast(F32).rearrange(
                     "p g (i u) -> p g i u", u=PAIR
                 ),
                 in_=turned[j][:].rearrange("p (g u) i -> p g i u", u=PAIR),
             )
 
-        def quantise(j):
-            codes[j] = work.tile([P, PASSES, P], U32, name="codes", align_bytes=64)
-            scales[j] = work.tile([P, PASSES, P], U8, name="scales", align_bytes=64)
+        def quantise(first, size):
+            c, s = divmod(first, TILES_PER_STORE)
+            tiles = slice(s, s + size)
             nc.vector.quantize_mx(
-                out=codes[j][:].rearrange("p g i -> p (g i)").bitcast(FP8X4),
-                scales=scales[j][:].rearrange("p g i -> p (g i)"),
-                in_=grouped[j][:].rearrange("p g i t -> p (g i t)"),
+                out=codes[c][:, tiles].rearrange("p s g i -> p (s g i)").bitcast(FP8X4),
+                scales=scales[c][:, tiles].rearrange("p s g i -> p (s g i)"),
+                in_=grouped[c][:, tiles].rearrange("p s g i t -> p (s g i t)"),
             )
 
         def project(j):
+            c, s = divmod(j, TILES_PER_STORE)
             y_ps[j] = psum_y.tile([P, MOVING_COLS], F32, name="y_ps")
             for g in range(PASSES):
                 nc.tensor.matmul_mx(
                     out=y_ps[j][:],
-                    lhsT=codes[j][:, g, :].bitcast(FP8X4),
-                    lhsT_scale=scales[j][:, g, :],
+                    lhsT=codes[c][:, s, g, :].bitcast(FP8X4),
+                    lhsT_scale=scales[c][:, s, g, :],
                     rhs=w_codes[:, g, :].bitcast(FP8X4),
                     rhs_scale=w_scales[:, g, :],
                     start=(g == 0),
@@ -226,7 +226,7 @@ def tile_ringattention_pa_t_kernel(tc, x, gamma, w_qkv, out_0, out_1, out_2):
             q_in = y_ps[j][:, 0:EMB].rearrange("p (h d) -> p h d", h=HEADS)
             kv_out = y_sb[group][:, 1:3, :, s, :]
             kv_in = y_ps[j][:, EMB:COLS].rearrange("p (j h d) -> p j h d", j=2, h=HEADS)
-            if j % 2 == 0:
+            if s == 3:
                 nc.vector.tensor_tensor(
                     out=y_sb[group][:, :, :, s, :],
                     in0=y_ps[j][:, 0:COLS].rearrange("p (j h d) -> p j h d", j=3, h=HEADS),
@@ -235,75 +235,107 @@ def tile_ringattention_pa_t_kernel(tc, x, gamma, w_qkv, out_0, out_1, out_2):
                 )
             else:
                 nc.scalar.mul(out=q_out, in_=q_in, mul=HEAD_DIM**-0.5)
-                nc.scalar.copy(out=kv_out, in_=kv_in)
+                (nc.vector.tensor_copy if s == 2 else nc.scalar.copy)(out=kv_out, in_=kv_in)
 
         def store(group):
             b, c = divmod(group, STORES_PER_BATCH)
             for tensor in range(3):
                 nc.sync.dma_start(out=out_views[tensor][b, c], in_=y_sb[group][:, tensor])
 
+        def interleave_weights(g):
+            nc.vector.tensor_copy(
+                out=w_grouped[:, g, 0:COLS, :], in_=w_raw[:, g].rearrange("p t n -> p n t")
+            )
+
+        def quantise_weights():
+            for g in range(PASSES):
+                nc.vector.quantize_mx(
+                    out=w_codes[:, g, :].bitcast(FP8X4),
+                    scales=w_scales[:, g, :],
+                    in_=w_grouped[:, g].rearrange("p n t -> p (n t)"),
+                )
+
+        for h in range(2):
+            load_rows(h)
         w_raw = setup.tile([P, PASSES, PACK, COLS], BF16)
-        nc.sync.dma_start(
-            out=w_raw[:].rearrange("p g t n -> p g (t n)"),
-            in_=w_qkv.rearrange("(g p t) n -> p g (t n)", p=P, t=PACK),
-        )
-        load_rows(0)
-        gamma_all = setup.tile([P, DIM], BF16)
-        nc.sync.dma_start(out=gamma_all[:], in_=gamma.partition_broadcast(P))
+        w_view = w_qkv.rearrange("(g p t) n -> g p (t n)", p=P, t=PACK)
+        for g in range(PASSES):
+            nc.sync.dma_start(out=w_raw[:, g].rearrange("p t n -> p (t n)"), in_=w_view[g])
+        for h in range(2, LOADS_AHEAD):
+            load_rows(h)
+        w_grouped = setup.tile([P, PASSES, MOVING_COLS, PACK], BF16, align_bytes=64)
+        w_codes = keep.tile([P, PASSES, MOVING_COLS], U32, align_bytes=64)
+        w_scales = keep.tile([P, PASSES, MOVING_COLS], U8, align_bytes=64)
         gamma_turned = keep.tile([P, PASSES, PACK], BF16)
-        nc.sync.dma_start(
+        nc.scalar.dma_start(
             out=gamma_turned[:], in_=gamma.rearrange("(g p t) -> p g t", p=P, t=PACK)
         )
-        for h in range(1, LOADS_AHEAD):
-            load_rows(h)
-        one = stat_pool.tile([P, 1], F32)
-        nc.vector.memset(one[:], 1.0)
-        warm = stat_pool.tile([P, 1], F32)
-        nc.scalar.activation(out=warm[:], in_=one[:], func=ACT.Abs_reciprocal_sqrt)
+        gamma_row = setup.tile([P, DIM], BF16)
+        nc.gpsimd.memset(gamma_row[:], 0.0)
+        nc.scalar.dma_start(out=gamma_row[0:1, :], in_=gamma.unsqueeze(0))
+        ones = setup.tile([P, P], BF16)
+        nc.vector.memset(ones[:], 1.0)
+        warm = setup.tile([P, 1], F32)
+        nc.scalar.activation(out=warm[:], in_=ones[:, 0:1], func=ACT.Abs_reciprocal_sqrt)
         identity = keep.tile([P, P], F32)
         make_identity(nc, identity[:])
-        identity_bf16 = setup.tile([P, P], BF16)
-        nc.vector.tensor_copy(out=identity_bf16[:], in_=identity[:])
         gamma_ps = psum_g.tile([P, DIM], BF16)
         for c in range(0, DIM, BANK):
             nc.tensor.matmul(
                 gamma_ps[:, c : c + BANK],
-                lhsT=identity_bf16[:],
-                rhs=gamma_all[:, c : c + BANK],
+                lhsT=ones[:],
+                rhs=gamma_row[:, c : c + BANK],
                 start=True,
                 stop=True,
             )
+        nc.vector.memset(w_grouped[:, :, COLS:MOVING_COLS, :], 0.0)
         y_factor = keep.tile([P, COLS], F32)
         nc.gpsimd.memset(y_factor[:, 0:EMB], HEAD_DIM**-0.5)
         nc.gpsimd.memset(y_factor[:, EMB:COLS], 1.0)
-        w_codes, w_scales = quantise_weights(nc, setup, keep, w_raw)
+
+        quantise_in_step = {}
+        first = 0
+        for size in QUANTISE_SIZES:
+            quantise_in_step[first + size - 1 + QUANTISE_LAG] = (first, size)
+            first += size
 
         def due(j):
             return 0 <= j < N_TILES
+
+        def load_done(j):
+            return due(j) and j % TILES_PER_LOAD == TILES_PER_LOAD - 1
+
+        def on_vector(j):
+            return j % TILES_PER_STORE == VECTOR_TILE
 
         for step in range(N_TILES + STORE_LAG):
             if step % TILES_PER_LOAD == 0 and step // TILES_PER_LOAD + LOADS_AHEAD < n_loads:
                 load_rows(step // TILES_PER_LOAD + LOADS_AHEAD)
             if due(step - STORE_LAG) and (step - STORE_LAG) % TILES_PER_STORE == TILES_PER_STORE - 1:
                 store((step - STORE_LAG) // TILES_PER_STORE)
-            if due(step - QUANTISE_LAG):
-                quantise(step - QUANTISE_LAG)
-            if due(step - CLAMP_LAG) and (step - CLAMP_LAG) % TILES_PER_LOAD == TILES_PER_LOAD - 1:
+            if step in quantise_in_step:
+                quantise(*quantise_in_step[step])
+            if load_done(step - CLAMP_LAG):
                 clamp((step - CLAMP_LAG) // TILES_PER_LOAD)
+            if step in WEIGHT_STEPS[:PASSES]:
+                interleave_weights(WEIGHT_STEPS.index(step))
+            if step == WEIGHT_STEPS[PASSES]:
+                quantise_weights()
+            if due(step - REGROUP_LAG):
+                j = step - REGROUP_LAG
+                open_group(j)
+                (regroup_words if on_vector(j) else regroup_times_gamma)(j)
             if due(step - EMIT_LAG):
                 emit(step - EMIT_LAG)
             if due(step - PROJECT_LAG):
                 project(step - PROJECT_LAG)
-            if due(step - REGROUP_LAG):
-                j = step - REGROUP_LAG
-                (regroup_odd if j % 2 else regroup_even)(j)
             if due(step - TURN_LAG):
                 j = step - TURN_LAG
-                (turn_odd if j % 2 else turn_even)(j)
+                (turn_words if on_vector(j) else turn_values)(j)
             if due(step - SCALE_LAG):
                 j = step - SCALE_LAG
-                (scale_odd if j % 2 else scale_even)(j)
-            if due(step - INVERT_LAG) and (step - INVERT_LAG) % TILES_PER_LOAD == TILES_PER_LOAD - 1:
+                (scale_on_vector if on_vector(j) else scale_on_gpsimd)(j)
+            if load_done(step - INVERT_LAG):
                 invert_norms((step - INVERT_LAG) // TILES_PER_LOAD)
             if due(step):
                 sum_squares(step)

@@ -14,6 +14,7 @@ ACT = mybir.ActivationFunctionType
 P = 128
 PACK = 4
 PAIR = 2
+LINE = 4
 K_PASS = P * PACK
 
 BATCH, SEQ, DIM, HEADS, HEAD_DIM = 4, 2048, 1024, 2, 64
@@ -45,7 +46,6 @@ QUANTISE_LAG = REGROUP_LAG + 2
 PROJECT_LAG = QUANTISE_LAG + 4
 EMIT_LAG = PROJECT_LAG + 1
 STORE_LAG = EMIT_LAG + 1
-WEIGHT_STEPS = (4, 5, 9)
 LOADS_AHEAD = 6
 
 
@@ -121,8 +121,8 @@ def tile_ringattention_pa_t_kernel(tc, x, gamma, w_qkv, out_0, out_1, out_2):
             h, s = divmod(j, TILES_PER_LOAD)
             scaled[j] = work.tile([P, PACK, DIM // PACK], F32, name="scaled")
             nc.gpsimd.tensor_scalar(
-                out=scaled[j][:],
-                in0=x_sb[h][:, s, :].rearrange("p (w t) -> p t w", t=PACK),
+                out=scaled[j][:].rearrange("p t (b w) -> p b t w", w=LINE),
+                in0=x_sb[h][:, s, :].rearrange("p (b w t) -> p b t w", t=PACK, w=LINE),
                 scalar1=row_scale[:, j : j + 1],
                 scalar2=0.0,
                 op0=ALU.mult,
@@ -179,8 +179,8 @@ def tile_ringattention_pa_t_kernel(tc, x, gamma, w_qkv, out_0, out_1, out_2):
             for g in range(PASSES):
                 nc.vector.tensor_tensor(
                     out=grouped[c][:, s, g],
-                    in0=turned[j][g][:].rearrange("p t i -> p i t"),
-                    in1=gamma_turned[:, g, :].unsqueeze(1).to_broadcast([P, P, PACK]),
+                    in0=gamma_turned[:, g, :].unsqueeze(1).to_broadcast([P, P, PACK]),
+                    in1=turned[j][g][:].rearrange("p t i -> p i t"),
                     op=ALU.mult,
                 )
 
@@ -229,13 +229,13 @@ def tile_ringattention_pa_t_kernel(tc, x, gamma, w_qkv, out_0, out_1, out_2):
             if s == 3:
                 nc.vector.tensor_tensor(
                     out=y_sb[group][:, :, :, s, :],
-                    in0=y_ps[j][:, 0:COLS].rearrange("p (j h d) -> p j h d", j=3, h=HEADS),
-                    in1=y_factor[:].rearrange("p (j h d) -> p j h d", j=3, h=HEADS),
+                    in0=y_factor[:].rearrange("p (j h d) -> p j h d", j=3, h=HEADS),
+                    in1=y_ps[j][:, 0:COLS].rearrange("p (j h d) -> p j h d", j=3, h=HEADS),
                     op=ALU.mult,
                 )
             else:
                 nc.scalar.mul(out=q_out, in_=q_in, mul=HEAD_DIM**-0.5)
-                (nc.vector.tensor_copy if s == 2 else nc.scalar.copy)(out=kv_out, in_=kv_in)
+                nc.scalar.copy(out=kv_out, in_=kv_in)
 
         def store(group):
             b, c = divmod(group, STORES_PER_BATCH)
@@ -255,28 +255,26 @@ def tile_ringattention_pa_t_kernel(tc, x, gamma, w_qkv, out_0, out_1, out_2):
                     in_=w_grouped[:, g].rearrange("p n t -> p (n t)"),
                 )
 
-        for h in range(2):
-            load_rows(h)
         w_raw = setup.tile([P, PASSES, PACK, COLS], BF16)
         w_view = w_qkv.rearrange("(g p t) n -> g p (t n)", p=P, t=PACK)
         for g in range(PASSES):
             nc.sync.dma_start(out=w_raw[:, g].rearrange("p t n -> p (t n)"), in_=w_view[g])
-        for h in range(2, LOADS_AHEAD):
+        for h in range(LOADS_AHEAD):
             load_rows(h)
         w_grouped = setup.tile([P, PASSES, MOVING_COLS, PACK], BF16, align_bytes=64)
         w_codes = keep.tile([P, PASSES, MOVING_COLS], U32, align_bytes=64)
         w_scales = keep.tile([P, PASSES, MOVING_COLS], U8, align_bytes=64)
         gamma_turned = keep.tile([P, PASSES, PACK], BF16)
+        ones = setup.tile([P, P], BF16)
+        nc.vector.memset(ones[:], 1.0)
+        warm = setup.tile([P, 1], F32)
+        nc.scalar.activation(out=warm[:], in_=ones[:, 0:1], func=ACT.Abs_reciprocal_sqrt)
         nc.scalar.dma_start(
             out=gamma_turned[:], in_=gamma.rearrange("(g p t) -> p g t", p=P, t=PACK)
         )
         gamma_row = setup.tile([P, DIM], BF16)
         nc.gpsimd.memset(gamma_row[:], 0.0)
         nc.scalar.dma_start(out=gamma_row[0:1, :], in_=gamma.unsqueeze(0))
-        ones = setup.tile([P, P], BF16)
-        nc.vector.memset(ones[:], 1.0)
-        warm = setup.tile([P, 1], F32)
-        nc.scalar.activation(out=warm[:], in_=ones[:, 0:1], func=ACT.Abs_reciprocal_sqrt)
         identity = keep.tile([P, P], F32)
         make_identity(nc, identity[:])
         gamma_ps = psum_g.tile([P, DIM], BF16)
@@ -292,6 +290,10 @@ def tile_ringattention_pa_t_kernel(tc, x, gamma, w_qkv, out_0, out_1, out_2):
         y_factor = keep.tile([P, COLS], F32)
         nc.gpsimd.memset(y_factor[:, 0:EMB], HEAD_DIM**-0.5)
         nc.gpsimd.memset(y_factor[:, EMB:COLS], 1.0)
+
+        for g in range(PASSES):
+            interleave_weights(g)
+        quantise_weights()
 
         quantise_in_step = {}
         first = 0
@@ -317,10 +319,6 @@ def tile_ringattention_pa_t_kernel(tc, x, gamma, w_qkv, out_0, out_1, out_2):
                 quantise(*quantise_in_step[step])
             if load_done(step - CLAMP_LAG):
                 clamp((step - CLAMP_LAG) // TILES_PER_LOAD)
-            if step in WEIGHT_STEPS[:PASSES]:
-                interleave_weights(WEIGHT_STEPS.index(step))
-            if step == WEIGHT_STEPS[PASSES]:
-                quantise_weights()
             if due(step - REGROUP_LAG):
                 j = step - REGROUP_LAG
                 open_group(j)

@@ -47,6 +47,9 @@ PROJECT_LAG = QUANTISE_LAG + 4
 EMIT_LAG = PROJECT_LAG + 1
 STORE_LAG = EMIT_LAG + 1
 LOADS_AHEAD = 6
+LOADS_FIRST = 2
+WEIGHT_STEPS = (SCALE_LAG, SCALE_LAG + 1, QUANTISE_LAG)
+EXTRA_Y = 12
 
 
 def tile_ringattention_pa_t_kernel(tc, x, gamma, w_qkv, out_0, out_1, out_2):
@@ -226,7 +229,7 @@ def tile_ringattention_pa_t_kernel(tc, x, gamma, w_qkv, out_0, out_1, out_2):
             q_in = y_ps[j][:, 0:EMB].rearrange("p (h d) -> p h d", h=HEADS)
             kv_out = y_sb[group][:, 1:3, :, s, :]
             kv_in = y_ps[j][:, EMB:COLS].rearrange("p (j h d) -> p j h d", j=2, h=HEADS)
-            if s == 3:
+            if s == 3 or j % EXTRA_Y == 1:
                 nc.vector.tensor_tensor(
                     out=y_sb[group][:, :, :, s, :],
                     in0=y_factor[:].rearrange("p (j h d) -> p j h d", j=3, h=HEADS),
@@ -237,10 +240,12 @@ def tile_ringattention_pa_t_kernel(tc, x, gamma, w_qkv, out_0, out_1, out_2):
                 nc.scalar.mul(out=q_out, in_=q_in, mul=HEAD_DIM**-0.5)
                 nc.scalar.copy(out=kv_out, in_=kv_in)
 
-        def store(group):
+        def store(group, tiles):
             b, c = divmod(group, STORES_PER_BATCH)
             for tensor in range(3):
-                nc.sync.dma_start(out=out_views[tensor][b, c], in_=y_sb[group][:, tensor])
+                nc.sync.dma_start(
+                    out=out_views[tensor][b, c][:, :, tiles], in_=y_sb[group][:, tensor, :, tiles]
+                )
 
         def interleave_weights(g):
             nc.vector.tensor_copy(
@@ -255,11 +260,13 @@ def tile_ringattention_pa_t_kernel(tc, x, gamma, w_qkv, out_0, out_1, out_2):
                     in_=w_grouped[:, g].rearrange("p n t -> p (n t)"),
                 )
 
+        for h in range(LOADS_FIRST):
+            load_rows(h)
         w_raw = setup.tile([P, PASSES, PACK, COLS], BF16)
         w_view = w_qkv.rearrange("(g p t) n -> g p (t n)", p=P, t=PACK)
         for g in range(PASSES):
             nc.sync.dma_start(out=w_raw[:, g].rearrange("p t n -> p (t n)"), in_=w_view[g])
-        for h in range(LOADS_AHEAD):
+        for h in range(LOADS_FIRST, LOADS_AHEAD):
             load_rows(h)
         w_grouped = setup.tile([P, PASSES, MOVING_COLS, PACK], BF16, align_bytes=64)
         w_codes = keep.tile([P, PASSES, MOVING_COLS], U32, align_bytes=64)
@@ -291,10 +298,6 @@ def tile_ringattention_pa_t_kernel(tc, x, gamma, w_qkv, out_0, out_1, out_2):
         nc.gpsimd.memset(y_factor[:, 0:EMB], HEAD_DIM**-0.5)
         nc.gpsimd.memset(y_factor[:, EMB:COLS], 1.0)
 
-        for g in range(PASSES):
-            interleave_weights(g)
-        quantise_weights()
-
         quantise_in_step = {}
         first = 0
         for size in QUANTISE_SIZES:
@@ -313,8 +316,13 @@ def tile_ringattention_pa_t_kernel(tc, x, gamma, w_qkv, out_0, out_1, out_2):
         for step in range(N_TILES + STORE_LAG):
             if step % TILES_PER_LOAD == 0 and step // TILES_PER_LOAD + LOADS_AHEAD < n_loads:
                 load_rows(step // TILES_PER_LOAD + LOADS_AHEAD)
-            if due(step - STORE_LAG) and (step - STORE_LAG) % TILES_PER_STORE == TILES_PER_STORE - 1:
-                store((step - STORE_LAG) // TILES_PER_STORE)
+            if due(step - STORE_LAG):
+                group, s = divmod(step - STORE_LAG, TILES_PER_STORE)
+                size = TILES_PER_STORE
+                if group == N_TILES // TILES_PER_STORE - 1:
+                    size = TILES_PER_STORE // 2
+                if s % size == size - 1:
+                    store(group, slice(s + 1 - size, s + 1))
             if step in quantise_in_step:
                 quantise(*quantise_in_step[step])
             if load_done(step - CLAMP_LAG):
@@ -333,6 +341,10 @@ def tile_ringattention_pa_t_kernel(tc, x, gamma, w_qkv, out_0, out_1, out_2):
             if due(step - SCALE_LAG):
                 j = step - SCALE_LAG
                 (scale_on_vector if on_vector(j) else scale_on_gpsimd)(j)
+            if step in WEIGHT_STEPS[:PASSES]:
+                interleave_weights(WEIGHT_STEPS.index(step))
+            if step == WEIGHT_STEPS[PASSES]:
+                quantise_weights()
             if load_done(step - INVERT_LAG):
                 invert_norms((step - INVERT_LAG) // TILES_PER_LOAD)
             if due(step):

@@ -29,6 +29,9 @@ TILES_PER_LOAD = 2
 STORES_PER_BATCH = SEQ // (P * TILES_PER_STORE)
 
 MOVING_COLS = 512
+WHOLE = (slice(0, MOVING_COLS),)
+SPLIT = (slice(0, 2 * EMB), slice(2 * EMB, COLS))
+FIRST_SPLIT = N_TILES - 12
 BANK = 512
 
 FLOPS = 2 * BATCH * SEQ * DIM * COLS
@@ -42,6 +45,7 @@ CLAMP_LAG = 3
 SCALE_LAG = CLAMP_LAG + 1
 TURN_LAG = SCALE_LAG + 1
 REGROUP_LAG = TURN_LAG + 2
+WORDS_LAG = TURN_LAG + 1
 QUANTISE_LAG = REGROUP_LAG + 2
 PROJECT_LAG = QUANTISE_LAG + 4
 EMIT_LAG = PROJECT_LAG + 1
@@ -49,7 +53,8 @@ STORE_LAG = EMIT_LAG + 1
 LOADS_AHEAD = 6
 LOADS_FIRST = 2
 WEIGHT_STEPS = (SCALE_LAG, SCALE_LAG + 1, QUANTISE_LAG)
-EXTRA_Y = 12
+VECTOR_Y = (1, 3, 7)
+LAST_VECTOR_Y = N_TILES - 16
 
 
 def tile_ringattention_pa_t_kernel(tc, x, gamma, w_qkv, out_0, out_1, out_2):
@@ -208,16 +213,17 @@ def tile_ringattention_pa_t_kernel(tc, x, gamma, w_qkv, out_0, out_1, out_2):
         def project(j):
             c, s = divmod(j, TILES_PER_STORE)
             y_ps[j] = psum_y.tile([P, MOVING_COLS], F32, name="y_ps")
-            for g in range(PASSES):
-                nc.tensor.matmul_mx(
-                    out=y_ps[j][:],
-                    lhsT=codes[c][:, s, g, :].bitcast(FP8X4),
-                    lhsT_scale=scales[c][:, s, g, :],
-                    rhs=w_codes[:, g, :].bitcast(FP8X4),
-                    rhs_scale=w_scales[:, g, :],
-                    start=(g == 0),
-                    stop=(g == PASSES - 1),
-                )
+            for cols in WHOLE if j < FIRST_SPLIT else SPLIT:
+                for g in range(PASSES):
+                    nc.tensor.matmul_mx(
+                        out=y_ps[j][:, cols],
+                        lhsT=codes[c][:, s, g, :].bitcast(FP8X4),
+                        lhsT_scale=scales[c][:, s, g, :],
+                        rhs=w_codes[:, g, cols].bitcast(FP8X4),
+                        rhs_scale=w_scales[:, g, cols],
+                        start=(g == 0),
+                        stop=(g == PASSES - 1),
+                    )
 
         def emit(j):
             group, s = divmod(j, TILES_PER_STORE)
@@ -229,7 +235,7 @@ def tile_ringattention_pa_t_kernel(tc, x, gamma, w_qkv, out_0, out_1, out_2):
             q_in = y_ps[j][:, 0:EMB].rearrange("p (h d) -> p h d", h=HEADS)
             kv_out = y_sb[group][:, 1:3, :, s, :]
             kv_in = y_ps[j][:, EMB:COLS].rearrange("p (j h d) -> p j h d", j=2, h=HEADS)
-            if s == 3 or j % EXTRA_Y == 1:
+            if j % 8 in VECTOR_Y and j < LAST_VECTOR_Y:
                 nc.vector.tensor_tensor(
                     out=y_sb[group][:, :, :, s, :],
                     in0=y_factor[:].rearrange("p (j h d) -> p j h d", j=3, h=HEADS),
@@ -260,7 +266,11 @@ def tile_ringattention_pa_t_kernel(tc, x, gamma, w_qkv, out_0, out_1, out_2):
                     in_=w_grouped[:, g].rearrange("p n t -> p (n t)"),
                 )
 
-        for h in range(LOADS_FIRST):
+        gamma_row = setup.tile([P, DIM], BF16)
+        nc.vector.memset(gamma_row[:].bitcast(U32), 0)
+        load_rows(0)
+        nc.sync.dma_start(out=gamma_row[0:1, :], in_=gamma.unsqueeze(0))
+        for h in range(1, LOADS_FIRST):
             load_rows(h)
         w_raw = setup.tile([P, PASSES, PACK, COLS], BF16)
         w_view = w_qkv.rearrange("(g p t) n -> g p (t n)", p=P, t=PACK)
@@ -279,9 +289,6 @@ def tile_ringattention_pa_t_kernel(tc, x, gamma, w_qkv, out_0, out_1, out_2):
         nc.scalar.dma_start(
             out=gamma_turned[:], in_=gamma.rearrange("(g p t) -> p g t", p=P, t=PACK)
         )
-        gamma_row = setup.tile([P, DIM], BF16)
-        nc.gpsimd.memset(gamma_row[:], 0.0)
-        nc.scalar.dma_start(out=gamma_row[0:1, :], in_=gamma.unsqueeze(0))
         identity = keep.tile([P, P], F32)
         make_identity(nc, identity[:])
         gamma_ps = psum_g.tile([P, DIM], BF16)
@@ -293,7 +300,7 @@ def tile_ringattention_pa_t_kernel(tc, x, gamma, w_qkv, out_0, out_1, out_2):
                 start=True,
                 stop=True,
             )
-        nc.vector.memset(w_grouped[:, :, COLS:MOVING_COLS, :], 0.0)
+        nc.gpsimd.memset(w_grouped[:, :, COLS:MOVING_COLS, :], 0.0)
         y_factor = keep.tile([P, COLS], F32)
         nc.gpsimd.memset(y_factor[:, 0:EMB], HEAD_DIM**-0.5)
         nc.gpsimd.memset(y_factor[:, EMB:COLS], 1.0)
@@ -330,7 +337,10 @@ def tile_ringattention_pa_t_kernel(tc, x, gamma, w_qkv, out_0, out_1, out_2):
             if due(step - REGROUP_LAG):
                 j = step - REGROUP_LAG
                 open_group(j)
-                (regroup_words if on_vector(j) else regroup_times_gamma)(j)
+                if not on_vector(j):
+                    regroup_times_gamma(j)
+            if due(step - WORDS_LAG) and on_vector(step - WORDS_LAG):
+                regroup_words(step - WORDS_LAG)
             if due(step - EMIT_LAG):
                 emit(step - EMIT_LAG)
             if due(step - PROJECT_LAG):

from contextlib import ExitStack

import concourse.mybir as mybir
from concourse.masks import make_identity

F32 = mybir.dt.float32
BF16 = mybir.dt.bfloat16
U32 = mybir.dt.uint32
U8 = mybir.dt.uint8
FP8X4 = mybir.dt.float8_e4m3fn_x4
ALU = mybir.AluOpType
ACT = mybir.ActivationFunctionType

P = 128
PACK = 4
PAIR = 2
LINE = 4
K_PASS = P * PACK

BATCH, SEQ, DIM, HEADS, HEAD_DIM = 4, 2048, 1024, 2, 64
EMB = HEADS * HEAD_DIM
COLS = 3 * EMB
PASSES = DIM // K_PASS
RMS_EPS = 1e-12
N_TILES = BATCH * SEQ // P

TILES_PER_STORE = 4
TILES_PER_LOAD = 2
STORES_PER_BATCH = SEQ // (P * TILES_PER_STORE)

MOVING_COLS = 512
WHOLE = (slice(0, MOVING_COLS),)
SPLIT = (slice(0, 2 * EMB), slice(2 * EMB, COLS))
FIRST_SPLIT = N_TILES - 12
BANK = 512

FLOPS = 2 * BATCH * SEQ * DIM * COLS


VECTOR_TILE = 2
QUANTISE_SIZES = [4] * (N_TILES // 4 - 1) + [1] * 4

INVERT_LAG = 1
CLAMP_LAG = 3
SCALE_LAG = CLAMP_LAG + 1
TURN_LAG = SCALE_LAG + 1
REGROUP_LAG = TURN_LAG + 2
WORDS_LAG = TURN_LAG + 1
QUANTISE_LAG = REGROUP_LAG + 2
PROJECT_LAG = QUANTISE_LAG + 4
EMIT_LAG = PROJECT_LAG + 1
STORE_LAG = EMIT_LAG + 1
LOADS_AHEAD = 6
LOADS_FIRST = 2
WEIGHT_STEPS = (SCALE_LAG, SCALE_LAG + 1, QUANTISE_LAG)
VECTOR_Y = (1, 3, 7)
LAST_VECTOR_Y = N_TILES - 16


def tile_ringattention_pa_t_kernel(tc, x, gamma, w_qkv, out_0, out_1, out_2):
    nc = tc.nc
    x_groups = x.rearrange("b (c p s) k -> (b c) p s k", p=P, s=TILES_PER_STORE)
    out_views = [
        o.rearrange("b h (c p s) d -> b c p h s d", p=P, s=TILES_PER_STORE)
        for o in (out_0, out_1, out_2)
    ]
    n_loads = N_TILES // TILES_PER_LOAD

    with ExitStack() as ctx:
        ctx.enter_context(tc.manual_schedule())
        setup = ctx.enter_context(tc.tile_pool(name="setup", bufs=1))
        keep = ctx.enter_context(tc.tile_pool(name="keep", bufs=1))
        x_pool = ctx.enter_context(tc.tile_pool(name="x", bufs=LOADS_AHEAD + 6))
        square_pool = ctx.enter_context(tc.tile_pool(name="square", bufs=2))
        work = ctx.enter_context(tc.tile_pool(name="work", bufs=4))
        y_pool = ctx.enter_context(tc.tile_pool(name="y", bufs=3))
        psum_g = ctx.enter_context(tc.psum_pool(name="psum_g", bufs=1))
        psum_t = ctx.enter_context(tc.psum_pool(name="psum_t", bufs=4))
        psum_y = ctx.enter_context(tc.psum_pool(name="psum_y", bufs=3))

        x_sb = {}
        scaled, normed, turned, grouped, codes, scales, y_ps, y_sb = ({} for i in range(8))

        sum_sq = keep.tile([P, N_TILES], F32)
        unclamped = keep.tile([P, N_TILES], F32)
        row_scale = keep.tile([P, N_TILES], F32)

        def rows_of(h):
            return slice(h * TILES_PER_LOAD, (h + 1) * TILES_PER_LOAD)

        def load_rows(h):
            group, half = divmod(h, TILES_PER_STORE // TILES_PER_LOAD)
            x_sb[h] = x_pool.tile([P, TILES_PER_LOAD, DIM], BF16, name="x_sb")
            s0 = half * TILES_PER_LOAD
            pieces = TILES_PER_LOAD if h == 0 else 1
            size = TILES_PER_LOAD // pieces
            for s in range(0, TILES_PER_LOAD, size):
                nc.sync.dma_start(
                    out=x_sb[h][:, s : s + size, :],
                    in_=x_groups[group][:, s0 + s : s0 + s + size, :],
                )

        def sum_squares(j):
            h, s = divmod(j, TILES_PER_LOAD)
            squares = square_pool.tile([P, DIM], BF16)
            nc.scalar.activation(
                out=squares[:],
                in_=x_sb[h][:, s, :],
                func=ACT.Square,
                accum_out=sum_sq[:, j : j + 1],
            )

        def invert_norms(h):
            nc.scalar.activation(
                out=unclamped[:, rows_of(h)],
                in_=sum_sq[:, rows_of(h)],
                func=ACT.Abs_reciprocal_sqrt,
                scale=1.0 / DIM,
            )

        def clamp(h):
            nc.vector.tensor_scalar_min(
                out=row_scale[:, rows_of(h)],
                in0=unclamped[:, rows_of(h)],
                scalar1=DIM**0.5 / RMS_EPS,
            )

        def scale_on_gpsimd(j):
            h, s = divmod(j, TILES_PER_LOAD)
            scaled[j] = work.tile([P, PACK, DIM // PACK], F32, name="scaled")
            nc.gpsimd.tensor_scalar(
                out=scaled[j][:].rearrange("p t (b w) -> p b t w", w=LINE),
                in0=x_sb[h][:, s, :].rearrange("p (b w t) -> p b t w", t=PACK, w=LINE),
                scalar1=row_scale[:, j : j + 1],
                scalar2=0.0,
                op0=ALU.mult,
                op1=ALU.add,
            )

        def scale_on_vector(j):
            h, s = divmod(j, TILES_PER_LOAD)
            normed[j] = work.tile([P, DIM], BF16, name="normed")
            nc.vector.scalar_tensor_tensor(
                out=normed[j][:],
                in0=x_sb[h][:, s, :],
                scalar=row_scale[:, j : j + 1],
                in1=gamma_ps[:],
                op0=ALU.mult,
                op1=ALU.mult,
            )

        def turn_values(j):
            turned[j] = []
            for g in range(PASSES):
                bank = psum_t.tile([P, PACK, P], F32, name="turned_bank")
                for t in range(PACK):
                    nc.tensor.transpose(
                        out=bank[:, t, :],
                        in_=scaled[j][:, t, g * P : (g + 1) * P],
                        identity=identity[:],
                    )
                turned[j].append(bank)

        def turn_words(j):
            words = normed[j][:].bitcast(F32)
            bank = psum_t.tile([P, PACK, P], F32, name="turned_bank")
            for g in range(PASSES):
                for u in range(PAIR):
                    w0 = g * PAIR * P
                    nc.tensor.transpose(
                        out=bank[:, g * PAIR + u, :],
                        in_=words[:, w0 + u : w0 + PAIR * P : PAIR],
                        identity=identity[:],
                    )
            turned[j] = bank

        def open_group(j):
            if j % TILES_PER_STORE == 0:
                c = j // TILES_PER_STORE
                shape = [P, TILES_PER_STORE, PASSES, P]
                grouped[c] = work.tile(shape + [PACK], BF16, name="grouped", align_bytes=64)
                codes[c] = work.tile(shape, U32, name="codes", align_bytes=64)
                scales[c] = work.tile(shape, U8, name="scales", align_bytes=64)

        def regroup_times_gamma(j):
            c, s = divmod(j, TILES_PER_STORE)
            for g in range(PASSES):
                nc.vector.tensor_tensor(
                    out=grouped[c][:, s, g],
                    in0=gamma_turned[:, g, :].unsqueeze(1).to_broadcast([P, P, PACK]),
                    in1=turned[j][g][:].rearrange("p t i -> p i t"),
                    op=ALU.mult,
                )

        def regroup_words(j):
            c, s = divmod(j, TILES_PER_STORE)
            nc.scalar.copy(
                out=grouped[c][:, s].rearrange("p g i t -> p g (i t)").bitcast(F32).rearrange(
                    "p g (i u) -> p g i u", u=PAIR
                ),
                in_=turned[j][:].rearrange("p (g u) i -> p g i u", u=PAIR),
            )

        def quantise(first, size):
            c, s = divmod(first, TILES_PER_STORE)
            tiles = slice(s, s + size)
            nc.vector.quantize_mx(
                out=codes[c][:, tiles].rearrange("p s g i -> p (s g i)").bitcast(FP8X4),
                scales=scales[c][:, tiles].rearrange("p s g i -> p (s g i)"),
                in_=grouped[c][:, tiles].rearrange("p s g i t -> p (s g i t)"),
            )

        def project(j):
            c, s = divmod(j, TILES_PER_STORE)
            y_ps[j] = psum_y.tile([P, MOVING_COLS], F32, name="y_ps")
            for cols in WHOLE if j < FIRST_SPLIT else SPLIT:
                for g in range(PASSES):
                    nc.tensor.matmul_mx(
                        out=y_ps[j][:, cols],
                        lhsT=codes[c][:, s, g, :].bitcast(FP8X4),
                        lhsT_scale=scales[c][:, s, g, :],
                        rhs=w_codes[:, g, cols].bitcast(FP8X4),
                        rhs_scale=w_scales[:, g, cols],
                        start=(g == 0),
                        stop=(g == PASSES - 1),
                    )

        def emit(j):
            group, s = divmod(j, TILES_PER_STORE)
            if s == 0:
                y_sb[group] = y_pool.tile(
                    [P, 3, HEADS, TILES_PER_STORE, HEAD_DIM], F32, name="y_sb"
                )
            q_out = y_sb[group][:, 0, :, s, :]
            q_in = y_ps[j][:, 0:EMB].rearrange("p (h d) -> p h d", h=HEADS)
            kv_out = y_sb[group][:, 1:3, :, s, :]
            kv_in = y_ps[j][:, EMB:COLS].rearrange("p (j h d) -> p j h d", j=2, h=HEADS)
            if j % 8 in VECTOR_Y and j < LAST_VECTOR_Y:
                nc.vector.tensor_tensor(
                    out=y_sb[group][:, :, :, s, :],
                    in0=y_factor[:].rearrange("p (j h d) -> p j h d", j=3, h=HEADS),
                    in1=y_ps[j][:, 0:COLS].rearrange("p (j h d) -> p j h d", j=3, h=HEADS),
                    op=ALU.mult,
                )
            else:
                nc.scalar.mul(out=q_out, in_=q_in, mul=HEAD_DIM**-0.5)
                nc.scalar.copy(out=kv_out, in_=kv_in)

        def store(group, tiles):
            b, c = divmod(group, STORES_PER_BATCH)
            for tensor in range(3):
                nc.sync.dma_start(
                    out=out_views[tensor][b, c][:, :, tiles], in_=y_sb[group][:, tensor, :, tiles]
                )

        def interleave_weights(g):
            nc.vector.tensor_copy(
                out=w_grouped[:, g, 0:COLS, :], in_=w_raw[:, g].rearrange("p t n -> p n t")
            )

        def quantise_weights():
            for g in range(PASSES):
                nc.vector.quantize_mx(
                    out=w_codes[:, g, :].bitcast(FP8X4),
                    scales=w_scales[:, g, :],
                    in_=w_grouped[:, g].rearrange("p n t -> p (n t)"),
                )

        gamma_row = setup.tile([P, DIM], BF16)
        nc.vector.memset(gamma_row[:].bitcast(U32), 0)
        load_rows(0)
        nc.sync.dma_start(out=gamma_row[0:1, :], in_=gamma.unsqueeze(0))
        for h in range(1, LOADS_FIRST):
            load_rows(h)
        w_raw = setup.tile([P, PASSES, PACK, COLS], BF16)
        w_view = w_qkv.rearrange("(g p t) n -> g p (t n)", p=P, t=PACK)
        for g in range(PASSES):
            nc.sync.dma_start(out=w_raw[:, g].rearrange("p t n -> p (t n)"), in_=w_view[g])
        for h in range(LOADS_FIRST, LOADS_AHEAD):
            load_rows(h)
        w_grouped = setup.tile([P, PASSES, MOVING_COLS, PACK], BF16, align_bytes=64)
        w_codes = keep.tile([P, PASSES, MOVING_COLS], U32, align_bytes=64)
        w_scales = keep.tile([P, PASSES, MOVING_COLS], U8, align_bytes=64)
        gamma_turned = keep.tile([P, PASSES, PACK], BF16)
        ones = setup.tile([P, P], BF16)
        nc.vector.memset(ones[:], 1.0)
        warm = setup.tile([P, 1], F32)
        nc.scalar.activation(out=warm[:], in_=ones[:, 0:1], func=ACT.Abs_reciprocal_sqrt)
        nc.scalar.dma_start(
            out=gamma_turned[:], in_=gamma.rearrange("(g p t) -> p g t", p=P, t=PACK)
        )
        identity = keep.tile([P, P], F32)
        make_identity(nc, identity[:])
        gamma_ps = psum_g.tile([P, DIM], BF16)
        for c in range(0, DIM, BANK):
            nc.tensor.matmul(
                gamma_ps[:, c : c + BANK],
                lhsT=ones[:],
                rhs=gamma_row[:, c : c + BANK],
                start=True,
                stop=True,
            )
        nc.gpsimd.memset(w_grouped[:, :, COLS:MOVING_COLS, :], 0.0)
        y_factor = keep.tile([P, COLS], F32)
        nc.gpsimd.memset(y_factor[:, 0:EMB], HEAD_DIM**-0.5)
        nc.gpsimd.memset(y_factor[:, EMB:COLS], 1.0)

        quantise_in_step = {}
        first = 0
        for size in QUANTISE_SIZES:
            quantise_in_step[first + size - 1 + QUANTISE_LAG] = (first, size)
            first += size

        def due(j):
            return 0 <= j < N_TILES

        def load_done(j):
            return due(j) and j % TILES_PER_LOAD == TILES_PER_LOAD - 1

        def on_vector(j):
            return j % TILES_PER_STORE == VECTOR_TILE

        for step in range(N_TILES + STORE_LAG):
            if step % TILES_PER_LOAD == 0 and step // TILES_PER_LOAD + LOADS_AHEAD < n_loads:
                load_rows(step // TILES_PER_LOAD + LOADS_AHEAD)
            if due(step - STORE_LAG):
                group, s = divmod(step - STORE_LAG, TILES_PER_STORE)
                size = TILES_PER_STORE
                if group == N_TILES // TILES_PER_STORE - 1:
                    size = TILES_PER_STORE // 2
                if s % size == size - 1:
                    store(group, slice(s + 1 - size, s + 1))
            if step in quantise_in_step:
                quantise(*quantise_in_step[step])
            if load_done(step - CLAMP_LAG):
                clamp((step - CLAMP_LAG) // TILES_PER_LOAD)
            if due(step - REGROUP_LAG):
                j = step - REGROUP_LAG
                open_group(j)
                if not on_vector(j):
                    regroup_times_gamma(j)
            if due(step - WORDS_LAG) and on_vector(step - WORDS_LAG):
                regroup_words(step - WORDS_LAG)
            if due(step - EMIT_LAG):
                emit(step - EMIT_LAG)
            if due(step - PROJECT_LAG):
                project(step - PROJECT_LAG)
            if due(step - TURN_LAG):
                j = step - TURN_LAG
                (turn_words if on_vector(j) else turn_values)(j)
            if due(step - SCALE_LAG):
                j = step - SCALE_LAG
                (scale_on_vector if on_vector(j) else scale_on_gpsimd)(j)
            if step in WEIGHT_STEPS[:PASSES]:
                interleave_weights(WEIGHT_STEPS.index(step))
            if step == WEIGHT_STEPS[PASSES]:
                quantise_weights()
            if load_done(step - INVERT_LAG):
                invert_norms((step - INVERT_LAG) // TILES_PER_LOAD)
            if due(step):
                sum_squares(step)
